import numpy as np
import ml_dtypes

BF16 = ml_dtypes.bfloat16


def bf(x):
    return np.asarray(x, np.float32).astype(BF16)


def f32(x):
    return np.asarray(x, np.float32)


def f64(x):
    return np.asarray(x).astype(np.float64)


def striped(idx):
    return np.tile(idx.reshape(-1, 16).T, (8, 1))


C, S, N, K, B, H1, E1, H2, E2, M = 1024, 2048, 8192, 8, 1024, 1024, 2048, 512, 1024, 256


def setup_inputs():
    emb = f32(0.5 * np.random.standard_normal((C, S)))
    w2 = bf(np.random.standard_normal((C, H1)) / np.sqrt(C))
    b2 = f32(0.1 * np.random.standard_normal((H1, 1)))
    w3 = bf(np.random.standard_normal((E1, H2)) / np.sqrt(E1))
    b3 = f32(0.1 * np.random.standard_normal((H2, 1)))
    w4 = bf(np.random.standard_normal((E2, M)) / np.sqrt(E2))
    idx = np.concatenate([np.random.permutation(S)[:B] for _ in range(K)])
    return {"emb": emb, "w2": w2, "b2": b2, "w3": w3, "b3": b3, "w4": w4, "offs": striped(idx)}


def reference(emb, w2, b2, w3, b3, w4, offs):
    idx = offs[:16].T.reshape(-1)
    acc = f64(emb)[:, idx].reshape(C, K, B).sum(axis=1)
    h = np.maximum(acc, 0.0)
    h = f64(w2).T @ h + f64(b2)
    h = np.maximum(np.concatenate((h, -h), axis=0), 0.0)
    h = f64(w3).T @ h + f64(b3)
    h = np.maximum(np.concatenate((h, -h), axis=0), 0.0)
    return f64(w4).T @ h

@@ -1,0 +1,116 @@
+import concourse.mybir as mybir
+from concourse.masks import make_identity
+
+F32, BF16, U16 = mybir.dt.float32, mybir.dt.bfloat16, mybir.dt.uint16
+ADD = mybir.AluOpType.add
+RELU = mybir.ActivationFunctionType.Relu
+
+P = 128
+C, S, K, B = 1024, 2048, 8, 1024
+H1, H2, M = 1024, 512, 256
+N = K * B
+BANK = 512
+CB, MB, QB, OB = C // P, H1 // P, H2 // P, M // P
+
+CHUNKS = (512, 512)
+
+FLOPS = 2 * B * (C * H1 + 2 * H1 * H2 + 2 * H2 * M)
+
+
+def tile_silknnue_b_kernel(tc, emb, w2, b2, w3, b3, w4, offs, out):
+    nc = tc.nc
+    with (
+        tc.tile_pool(name="held", bufs=1) as held,
+        tc.tile_pool(name="steps", bufs=3) as steps,
+        tc.tile_pool(name="sums", bufs=8) as sums,
+        tc.tile_pool(name="acts", bufs=2) as acts,
+        tc.psum_pool(name="psum", bufs=8) as psum,
+    ):
+        offsets = held.tile([P, N // 16], U16, name="offsets")
+        nc.sync.dma_start(offsets[:], offs)
+        tables = [held.tile([P, S], F32, name=f"table{cb}") for cb in range(CB)]
+        w2_sb = held.tile([P, CB, H1], BF16, name="w2_sb")
+        w3_sb = held.tile([P, 2 * MB, H2], BF16, name="w3_sb")
+        w4_sb = held.tile([P, 2 * QB, M], BF16, name="w4_sb")
+        bias_rows = held.tile([P, P], F32, name="bias_rows")
+        nc.gpsimd.memset(bias_rows[:], 0.0)
+        for cb in range(CB):
+            nc.sync.dma_start(tables[cb][:], emb[cb * P : (cb + 1) * P, :])
+            if cb == 1:
+                nc.sync.dma_start(w2_sb[:], w2.rearrange("(cb p) m -> p cb m", p=P))
+                nc.sync.dma_start(bias_rows[0:MB, :], b2.rearrange("(mb p) o -> mb (p o)", p=P))
+                nc.sync.dma_start(bias_rows[MB : MB + QB, :], b3.rearrange("(qb p) o -> qb (p o)", p=P))
+        nc.sync.dma_start(w3_sb[:], w3.rearrange("(e p) q -> p e q", p=P))
+        nc.sync.dma_start(w4_sb[:], w4.rearrange("(e p) o -> p e o", p=P))
+
+        zeros = held.tile([P, BANK], F32, name="zeros")
+        nc.gpsimd.memset(zeros[:], 0.0)
+        identity = held.tile([P, P], F32, name="identity")
+        make_identity(nc, identity[:])
+        flipped = psum.tile([P, BANK], F32, name="flipped", tag="bank")
+        nc.tensor.transpose(flipped[:, 0:P], bias_rows[:], identity[:])
+        bias = held.tile([P, MB + QB], F32, name="bias")
+        neg_bias = held.tile([P, MB + QB], F32, name="neg_bias")
+        nc.scalar.copy(bias[:], flipped[:, 0 : MB + QB])
+        nc.scalar.mul(neg_bias[:], flipped[:, 0 : MB + QB], -1.0)
+
+        def paired_relu(pos, neg, bank, j, w):
+            nc.scalar.activation(pos[:, :w], bank[:, :w], RELU, bias=bias[:, j : j + 1], scale=1.0)
+            nc.scalar.activation(neg[:, :w], bank[:, :w], RELU, bias=neg_bias[:, j : j + 1], scale=-1.0)
+
+        p0 = 0
+        for w in CHUNKS:
+            h1 = [psum.tile([P, BANK], F32, name=f"h1_{mb}", tag="bank") for mb in range(MB)]
+            for cb in range(CB):
+                acc = zeros
+                for k in range(K):
+                    first = (k * B + p0) // 16
+                    picked = tables[cb][:].indirect(offsets[:, first : first + w // 16])
+                    if k < K - 1:
+                        longer = steps.tile([P, BANK], F32, name="partial")
+                    else:
+                        longer = sums.tile([P, BANK], F32, name="total")
+                    nc.vector.tensor_tensor(longer[:, :w], picked, acc[:, :w], ADD)
+                    acc = longer
+                r = acts.tile([P, BANK], BF16, name=f"r{cb}")
+                nc.scalar.activation(r[:, :w], acc[:, :w], RELU)
+                for mb in range(MB):
+                    nc.tensor.matmul(
+                        h1[mb][:, :w],
+                        w2_sb[:, cb, mb * P : (mb + 1) * P],
+                        r[:, :w],
+                        start=(cb == 0),
+                        stop=(cb == CB - 1),
+                    )
+
+            u1 = [acts.tile([P, BANK], BF16, name=f"u1_{e}") for e in range(2 * MB)]
+            for mb in range(MB):
+                paired_relu(u1[mb], u1[MB + mb], h1[mb], mb, w)
+            h2 = [psum.tile([P, BANK], F32, name=f"h2_{qb}", tag="bank") for qb in range(QB)]
+            for e in range(2 * MB):
+                for qb in range(QB):
+                    nc.tensor.matmul(
+                        h2[qb][:, :w],
+                        w3_sb[:, e, qb * P : (qb + 1) * P],
+                        u1[e][:, :w],
+                        start=(e == 0),
+                        stop=(e == 2 * MB - 1),
+                    )
+
+            u2 = [acts.tile([P, BANK], BF16, name=f"u2_{e}") for e in range(2 * QB)]
+            for qb in range(QB):
+                paired_relu(u2[qb], u2[QB + qb], h2[qb], MB + qb, w)
+            for ob in range(OB):
+                y = psum.tile([P, BANK], F32, name="y", tag="bank")
+                for e in range(2 * QB):
+                    nc.tensor.matmul(
+                        y[:, :w],
+                        w4_sb[:, e, ob * P : (ob + 1) * P],
+                        u2[e][:, :w],
+                        start=(e == 0),
+                        stop=(e == 2 * QB - 1),
+                    )
+                y_sb = acts.tile([P, BANK], F32, name="y_sb")
+                nc.scalar.copy(y_sb[:, :w], y[:, :w])
+                nc.sync.dma_start(out[ob * P : (ob + 1) * P, p0 : p0 + w], y_sb[:, :w])
+            p0 += w

@@ -13,6 +13,7 @@ BANK = 512
 CB, MB, QB, OB = C // P, H1 // P, H2 // P, M // P
 
 CHUNKS = (512, 512)
+LANES = 2
 
 FLOPS = 2 * B * (C * H1 + 2 * H1 * H2 + 2 * H2 * M)
 
@@ -21,7 +22,7 @@ def tile_silknnue_b_kernel(tc, emb, w2, b2, w3, b3, w4, offs, out):
     nc = tc.nc
     with (
         tc.tile_pool(name="held", bufs=1) as held,
-        tc.tile_pool(name="steps", bufs=3) as steps,
+        tc.tile_pool(name="steps", bufs=3 * LANES) as steps,
         tc.tile_pool(name="sums", bufs=8) as sums,
         tc.tile_pool(name="acts", bufs=2) as acts,
         tc.psum_pool(name="psum", bufs=8) as psum,
@@ -61,27 +62,30 @@ def tile_silknnue_b_kernel(tc, emb, w2, b2, w3, b3, w4, offs, out):
         p0 = 0
         for w in CHUNKS:
             h1 = [psum.tile([P, BANK], F32, name=f"h1_{mb}", tag="bank") for mb in range(MB)]
-            for cb in range(CB):
-                acc = zeros
+            for cb0 in range(0, CB, LANES):
+                lanes = range(cb0, cb0 + LANES)
+                acc = {cb: zeros for cb in lanes}
                 for k in range(K):
                     first = (k * B + p0) // 16
-                    picked = tables[cb][:].indirect(offsets[:, first : first + w // 16])
-                    if k < K - 1:
-                        longer = steps.tile([P, BANK], F32, name="partial")
-                    else:
-                        longer = sums.tile([P, BANK], F32, name="total")
-                    nc.vector.tensor_tensor(longer[:, :w], picked, acc[:, :w], ADD)
-                    acc = longer
-                r = acts.tile([P, BANK], BF16, name=f"r{cb}")
-                nc.scalar.activation(r[:, :w], acc[:, :w], RELU)
-                for mb in range(MB):
-                    nc.tensor.matmul(
-                        h1[mb][:, :w],
-                        w2_sb[:, cb, mb * P : (mb + 1) * P],
-                        r[:, :w],
-                        start=(cb == 0),
-                        stop=(cb == CB - 1),
-                    )
+                    for cb in lanes:
+                        picked = tables[cb][:].indirect(offsets[:, first : first + w // 16])
+                        if k < K - 1:
+                            longer = steps.tile([P, BANK], F32, name="partial")
+                        else:
+                            longer = sums.tile([P, BANK], F32, name="total")
+                        nc.vector.tensor_tensor(longer[:, :w], picked, acc[cb][:, :w], ADD)
+                        acc[cb] = longer
+                for cb in lanes:
+                    r = acts.tile([P, BANK], BF16, name=f"r{cb}")
+                    nc.scalar.activation(r[:, :w], acc[cb][:, :w], RELU)
+                    for mb in range(MB):
+                        nc.tensor.matmul(
+                            h1[mb][:, :w],
+                            w2_sb[:, cb, mb * P : (mb + 1) * P],
+                            r[:, :w],
+                            start=(cb == 0),
+                            stop=(cb == CB - 1),
+                        )
 
             u1 = [acts.tile([P, BANK], BF16, name=f"u1_{e}") for e in range(2 * MB)]
             for mb in range(MB):

@@ -12,7 +12,8 @@ N = K * B
 BANK = 512
 CB, MB, QB, OB = C // P, H1 // P, H2 // P, M // P
 
-CHUNKS = (512, 512)
+CHUNKS = (384, 320, 192, 128)
+assert sum(CHUNKS) == B and max(CHUNKS) <= BANK
 LANES = 2
 
 FLOPS = 2 * B * (C * H1 + 2 * H1 * H2 + 2 * H2 * M)
@@ -23,8 +24,9 @@ def tile_silknnue_b_kernel(tc, emb, w2, b2, w3, b3, w4, offs, out):
     with (
         tc.tile_pool(name="held", bufs=1) as held,
         tc.tile_pool(name="steps", bufs=3 * LANES) as steps,
-        tc.tile_pool(name="sums", bufs=8) as sums,
+        tc.tile_pool(name="sums", bufs=CB) as sums,
         tc.tile_pool(name="acts", bufs=2) as acts,
+        tc.tile_pool(name="turns", bufs=1) as turns,
         tc.psum_pool(name="psum", bufs=8) as psum,
     ):
         offsets = held.tile([P, N // 16], U16, name="offsets")
@@ -37,7 +39,7 @@ def tile_silknnue_b_kernel(tc, emb, w2, b2, w3, b3, w4, offs, out):
         nc.gpsimd.memset(bias_rows[:], 0.0)
         for cb in range(CB):
             nc.sync.dma_start(tables[cb][:], emb[cb * P : (cb + 1) * P, :])
-            if cb == 1:
+            if cb == LANES - 1:
                 nc.sync.dma_start(w2_sb[:], w2.rearrange("(cb p) m -> p cb m", p=P))
                 nc.sync.dma_start(bias_rows[0:MB, :], b2.rearrange("(mb p) o -> mb (p o)", p=P))
                 nc.sync.dma_start(bias_rows[MB : MB + QB, :], b3.rearrange("(qb p) o -> qb (p o)", p=P))
@@ -61,6 +63,8 @@ def tile_silknnue_b_kernel(tc, emb, w2, b2, w3, b3, w4, offs, out):
 
         p0 = 0
         for w in CHUNKS:
+            last = p0 + w == B
+
             h1 = [psum.tile([P, BANK], F32, name=f"h1_{mb}", tag="bank") for mb in range(MB)]
             for cb0 in range(0, CB, LANES):
                 lanes = range(cb0, cb0 + LANES)
@@ -76,7 +80,7 @@ def tile_silknnue_b_kernel(tc, emb, w2, b2, w3, b3, w4, offs, out):
                         nc.vector.tensor_tensor(longer[:, :w], picked, acc[cb][:, :w], ADD)
                         acc[cb] = longer
                 for cb in lanes:
-                    r = acts.tile([P, BANK], BF16, name=f"r{cb}")
+                    r = turns.tile([P, BANK], BF16, name=f"r{cb}", tag=f"turn{cb}")
                     nc.scalar.activation(r[:, :w], acc[cb][:, :w], RELU)
                     for mb in range(MB):
                         nc.tensor.matmul(
@@ -90,31 +94,39 @@ def tile_silknnue_b_kernel(tc, emb, w2, b2, w3, b3, w4, offs, out):
             u1 = [acts.tile([P, BANK], BF16, name=f"u1_{e}") for e in range(2 * MB)]
             for mb in range(MB):
                 paired_relu(u1[mb], u1[MB + mb], h1[mb], mb, w)
-            h2 = [psum.tile([P, BANK], F32, name=f"h2_{qb}", tag="bank") for qb in range(QB)]
-            for e in range(2 * MB):
-                for qb in range(QB):
-                    nc.tensor.matmul(
-                        h2[qb][:, :w],
-                        w3_sb[:, e, qb * P : (qb + 1) * P],
-                        u1[e][:, :w],
-                        start=(e == 0),
-                        stop=(e == 2 * MB - 1),
-                    )
 
-            u2 = [acts.tile([P, BANK], BF16, name=f"u2_{e}") for e in range(2 * QB)]
+            u2 = [turns.tile([P, BANK], BF16, name=f"u2_{e}", tag=f"turn{e}") for e in range(2 * QB)]
+            for half in (range(0, QB // 2), range(QB // 2, QB)):
+                h2 = {qb: psum.tile([P, BANK], F32, name=f"h2_{qb}", tag="bank") for qb in half}
+                for mb in range(MB):
+                    for e in (mb, MB + mb):
+                        for qb in half:
+                            nc.tensor.matmul(
+                                h2[qb][:, :w],
+                                w3_sb[:, e, qb * P : (qb + 1) * P],
+                                u1[e][:, :w],
+                                start=(e == 0),
+                                stop=(e == 2 * MB - 1),
+                            )
+                for qb in half:
+                    paired_relu(u2[qb], u2[QB + qb], h2[qb], MB + qb, w)
+
+            y = [psum.tile([P, BANK], F32, name=f"y{ob}", tag="bank") for ob in range(OB)]
             for qb in range(QB):
-                paired_relu(u2[qb], u2[QB + qb], h2[qb], MB + qb, w)
+                for e in (qb, QB + qb):
+                    for ob in range(OB):
+                        nc.tensor.matmul(
+                            y[ob][:, :w],
+                            w4_sb[:, e, ob * P : (ob + 1) * P],
+                            u2[e][:, :w],
+                            start=(e == 0),
+                            stop=(e == 2 * QB - 1),
+                        )
             for ob in range(OB):
-                y = psum.tile([P, BANK], F32, name="y", tag="bank")
-                for e in range(2 * QB):
-                    nc.tensor.matmul(
-                        y[:, :w],
-                        w4_sb[:, e, ob * P : (ob + 1) * P],
-                        u2[e][:, :w],
-                        start=(e == 0),
-                        stop=(e == 2 * QB - 1),
-                    )
-                y_sb = acts.tile([P, BANK], F32, name="y_sb")
-                nc.scalar.copy(y_sb[:, :w], y[:, :w])
+                y_sb = acts.tile([P, BANK], F32, name=f"y_sb{ob}")
+                if last and ob == 0:
+                    nc.vector.tensor_copy(y_sb[:, :w], y[ob][:, :w])
+                else:
+                    nc.scalar.copy(y_sb[:, :w], y[ob][:, :w])
                 nc.sync.dma_start(out[ob * P : (ob + 1) * P, p0 : p0 + w], y_sb[:, :w])
             p0 += w

@@ -12,7 +12,7 @@ N = K * B
 BANK = 512
 CB, MB, QB, OB = C // P, H1 // P, H2 // P, M // P
 
-CHUNKS = (384, 320, 192, 128)
+CHUNKS = (512, 352, 160)
 assert sum(CHUNKS) == B and max(CHUNKS) <= BANK
 LANES = 2
 
@@ -66,6 +66,7 @@ def tile_silknnue_b_kernel(tc, emb, w2, b2, w3, b3, w4, offs, out):
             last = p0 + w == B
 
             h1 = [psum.tile([P, BANK], F32, name=f"h1_{mb}", tag="bank") for mb in range(MB)]
+            r = turns.tile([P, CB, BANK], BF16, name="r", tag="turn")
             for cb0 in range(0, CB, LANES):
                 lanes = range(cb0, cb0 + LANES)
                 acc = {cb: zeros for cb in lanes}
@@ -80,13 +81,12 @@ def tile_silknnue_b_kernel(tc, emb, w2, b2, w3, b3, w4, offs, out):
                         nc.vector.tensor_tensor(longer[:, :w], picked, acc[cb][:, :w], ADD)
                         acc[cb] = longer
                 for cb in lanes:
-                    r = turns.tile([P, BANK], BF16, name=f"r{cb}", tag=f"turn{cb}")
-                    nc.scalar.activation(r[:, :w], acc[cb][:, :w], RELU)
+                    nc.scalar.activation(r[:, cb, :w], acc[cb][:, :w], RELU)
                     for mb in range(MB):
                         nc.tensor.matmul(
                             h1[mb][:, :w],
                             w2_sb[:, cb, mb * P : (mb + 1) * P],
-                            r[:, :w],
+                            r[:, cb, :w],
                             start=(cb == 0),
                             stop=(cb == CB - 1),
                         )
@@ -95,7 +95,7 @@ def tile_silknnue_b_kernel(tc, emb, w2, b2, w3, b3, w4, offs, out):
             for mb in range(MB):
                 paired_relu(u1[mb], u1[MB + mb], h1[mb], mb, w)
 
-            u2 = [turns.tile([P, BANK], BF16, name=f"u2_{e}", tag=f"turn{e}") for e in range(2 * QB)]
+            u2 = turns.tile([P, 2 * QB, BANK], BF16, name="u2", tag="turn")
             for half in (range(0, QB // 2), range(QB // 2, QB)):
                 h2 = {qb: psum.tile([P, BANK], F32, name=f"h2_{qb}", tag="bank") for qb in half}
                 for mb in range(MB):
@@ -109,7 +109,7 @@ def tile_silknnue_b_kernel(tc, emb, w2, b2, w3, b3, w4, offs, out):
                                 stop=(e == 2 * MB - 1),
                             )
                 for qb in half:
-                    paired_relu(u2[qb], u2[QB + qb], h2[qb], MB + qb, w)
+                    paired_relu(u2[:, qb, :], u2[:, QB + qb, :], h2[qb], MB + qb, w)
 
             y = [psum.tile([P, BANK], F32, name=f"y{ob}", tag="bank") for ob in range(OB)]
             for qb in range(QB):
@@ -118,7 +118,7 @@ def tile_silknnue_b_kernel(tc, emb, w2, b2, w3, b3, w4, offs, out):
                         nc.tensor.matmul(
                             y[ob][:, :w],
                             w4_sb[:, e, ob * P : (ob + 1) * P],
-                            u2[e][:, :w],
+                            u2[:, e, :w],
                             start=(e == 0),
                             stop=(e == 2 * QB - 1),
                         )

@@ -12,8 +12,9 @@ N = K * B
 BANK = 512
 CB, MB, QB, OB = C // P, H1 // P, H2 // P, M // P
 
-CHUNKS = (512, 352, 160)
-assert sum(CHUNKS) == B and max(CHUNKS) <= BANK
+GROUPS = ((512, 96), (288,), (128,))
+WIDEST = max(sum(group) for group in GROUPS)
+assert sum(sum(group) for group in GROUPS) == B and max(max(group) for group in GROUPS) <= BANK
 LANES = 2
 
 FLOPS = 2 * B * (C * H1 + 2 * H1 * H2 + 2 * H2 * M)
@@ -24,7 +25,7 @@ def tile_silknnue_b_kernel(tc, emb, w2, b2, w3, b3, w4, offs, out):
     with (
         tc.tile_pool(name="held", bufs=1) as held,
         tc.tile_pool(name="steps", bufs=3 * LANES) as steps,
-        tc.tile_pool(name="sums", bufs=CB) as sums,
+        tc.tile_pool(name="sums", bufs=2 * CB) as sums,
         tc.tile_pool(name="acts", bufs=2) as acts,
         tc.tile_pool(name="turns", bufs=1) as turns,
         tc.psum_pool(name="psum", bufs=8) as psum,
@@ -46,7 +47,7 @@ def tile_silknnue_b_kernel(tc, emb, w2, b2, w3, b3, w4, offs, out):
         nc.sync.dma_start(w3_sb[:], w3.rearrange("(e p) q -> p e q", p=P))
         nc.sync.dma_start(w4_sb[:], w4.rearrange("(e p) o -> p e o", p=P))
 
-        zeros = held.tile([P, BANK], F32, name="zeros")
+        zeros = held.tile([P, WIDEST], F32, name="zeros")
         nc.gpsimd.memset(zeros[:], 0.0)
         identity = held.tile([P, P], F32, name="identity")
         make_identity(nc, identity[:])
@@ -57,40 +58,22 @@ def tile_silknnue_b_kernel(tc, emb, w2, b2, w3, b3, w4, offs, out):
         nc.scalar.copy(bias[:], flipped[:, 0 : MB + QB])
         nc.scalar.mul(neg_bias[:], flipped[:, 0 : MB + QB], -1.0)
 
+        def layer1(h1, r, total, cb, c0, w):
+            nc.scalar.activation(r[:, cb, :w], total[:, c0 : c0 + w], RELU)
+            for mb in range(MB):
+                nc.tensor.matmul(
+                    h1[mb][:, :w],
+                    w2_sb[:, cb, mb * P : (mb + 1) * P],
+                    r[:, cb, :w],
+                    start=(cb == 0),
+                    stop=(cb == CB - 1),
+                )
+
         def paired_relu(pos, neg, bank, j, w):
             nc.scalar.activation(pos[:, :w], bank[:, :w], RELU, bias=bias[:, j : j + 1], scale=1.0)
             nc.scalar.activation(neg[:, :w], bank[:, :w], RELU, bias=neg_bias[:, j : j + 1], scale=-1.0)
 
-        p0 = 0
-        for w in CHUNKS:
-            last = p0 + w == B
-
-            h1 = [psum.tile([P, BANK], F32, name=f"h1_{mb}", tag="bank") for mb in range(MB)]
-            r = turns.tile([P, CB, BANK], BF16, name="r", tag="turn")
-            for cb0 in range(0, CB, LANES):
-                lanes = range(cb0, cb0 + LANES)
-                acc = {cb: zeros for cb in lanes}
-                for k in range(K):
-                    first = (k * B + p0) // 16
-                    for cb in lanes:
-                        picked = tables[cb][:].indirect(offsets[:, first : first + w // 16])
-                        if k < K - 1:
-                            longer = steps.tile([P, BANK], F32, name="partial")
-                        else:
-                            longer = sums.tile([P, BANK], F32, name="total")
-                        nc.vector.tensor_tensor(longer[:, :w], picked, acc[cb][:, :w], ADD)
-                        acc[cb] = longer
-                for cb in lanes:
-                    nc.scalar.activation(r[:, cb, :w], acc[cb][:, :w], RELU)
-                    for mb in range(MB):
-                        nc.tensor.matmul(
-                            h1[mb][:, :w],
-                            w2_sb[:, cb, mb * P : (mb + 1) * P],
-                            r[:, cb, :w],
-                            start=(cb == 0),
-                            stop=(cb == CB - 1),
-                        )
-
+        def after_layer1(h1, p0, w):
             u1 = [acts.tile([P, BANK], BF16, name=f"u1_{e}") for e in range(2 * MB)]
             for mb in range(MB):
                 paired_relu(u1[mb], u1[MB + mb], h1[mb], mb, w)
@@ -124,9 +107,43 @@ def tile_silknnue_b_kernel(tc, emb, w2, b2, w3, b3, w4, offs, out):
                         )
             for ob in range(OB):
                 y_sb = acts.tile([P, BANK], F32, name=f"y_sb{ob}")
-                if last and ob == 0:
+                if p0 + w == B and ob == 0:
                     nc.vector.tensor_copy(y_sb[:, :w], y[ob][:, :w])
                 else:
                     nc.scalar.copy(y_sb[:, :w], y[ob][:, :w])
                 nc.sync.dma_start(out[ob * P : (ob + 1) * P, p0 : p0 + w], y_sb[:, :w])
-            p0 += w
+
+        p0 = 0
+        for group in GROUPS:
+            gw = sum(group)
+
+            h1 = [psum.tile([P, BANK], F32, name=f"h1_{mb}", tag="bank") for mb in range(MB)]
+            r = turns.tile([P, CB, BANK], BF16, name="r", tag="turn")
+            totals = {}
+            for cb0 in range(0, CB, LANES):
+                lanes = range(cb0, cb0 + LANES)
+                acc = {cb: zeros for cb in lanes}
+                for k in range(K):
+                    first = (k * B + p0) // 16
+                    for cb in lanes:
+                        picked = tables[cb][:].indirect(offsets[:, first : first + gw // 16])
+                        if k < K - 1:
+                            longer = steps.tile([P, WIDEST], F32, name="partial")
+                        else:
+                            longer = sums.tile([P, WIDEST], F32, name="total")
+                        nc.vector.tensor_tensor(longer[:, :gw], picked, acc[cb][:, :gw], ADD)
+                        acc[cb] = longer
+                for cb in lanes:
+                    totals[cb] = acc[cb]
+                    layer1(h1, r, totals[cb], cb, 0, group[0])
+            after_layer1(h1, p0, group[0])
+
+            c0 = group[0]
+            for w in group[1:]:
+                h1 = [psum.tile([P, BANK], F32, name=f"h1_{mb}", tag="bank") for mb in range(MB)]
+                r = turns.tile([P, CB, BANK], BF16, name="r", tag="turn")
+                for cb in range(CB):
+                    layer1(h1, r, totals[cb], cb, c0, w)
+                after_layer1(h1, p0 + c0, w)
+                c0 += w
+            p0 += gw

@@ -79,20 +79,30 @@ def tile_silknnue_b_kernel(tc, emb, w2, b2, w3, b3, w4, offs, out):
                 paired_relu(u1[mb], u1[MB + mb], h1[mb], mb, w)
 
             u2 = turns.tile([P, 2 * QB, BANK], BF16, name="u2", tag="turn")
-            for half in (range(0, QB // 2), range(QB // 2, QB)):
-                h2 = {qb: psum.tile([P, BANK], F32, name=f"h2_{qb}", tag="bank") for qb in half}
-                for mb in range(MB):
-                    for e in (mb, MB + mb):
-                        for qb in half:
-                            nc.tensor.matmul(
-                                h2[qb][:, :w],
-                                w3_sb[:, e, qb * P : (qb + 1) * P],
-                                u1[e][:, :w],
-                                start=(e == 0),
-                                stop=(e == 2 * MB - 1),
-                            )
-                for qb in half:
-                    paired_relu(u2[:, qb, :], u2[:, QB + qb, :], h2[qb], MB + qb, w)
+            ready_order = [e for mb in range(MB) for e in (mb, MB + mb)]
+            h2 = {}
+
+            def layer2(e, qb):
+                nc.tensor.matmul(
+                    h2[qb][:, :w],
+                    w3_sb[:, e, qb * P : (qb + 1) * P],
+                    u1[e][:, :w],
+                    start=(e == ready_order[0]),
+                    stop=(e == ready_order[-1]),
+                )
+
+            for qb in range(0, QB // 2):
+                h2[qb] = psum.tile([P, BANK], F32, name=f"h2_{qb}", tag="bank")
+            for e in ready_order:
+                for qb in range(0, QB // 2):
+                    layer2(e, qb)
+            for qb in range(0, QB // 2):
+                paired_relu(u2[:, qb, :], u2[:, QB + qb, :], h2[qb], MB + qb, w)
+            for qb in range(QB // 2, QB):
+                h2[qb] = psum.tile([P, BANK], F32, name=f"h2_{qb}", tag="bank")
+                for e in ready_order:
+                    layer2(e, qb)
+                paired_relu(u2[:, qb, :], u2[:, QB + qb, :], h2[qb], MB + qb, w)
 
             y = [psum.tile([P, BANK], F32, name=f"y{ob}", tag="bank") for ob in range(OB)]
             for qb in range(QB):

@@ -1,5 +1,4 @@
 import concourse.mybir as mybir
-from concourse.masks import make_identity
 
 F32, BF16, U16 = mybir.dt.float32, mybir.dt.bfloat16, mybir.dt.uint16
 ADD = mybir.AluOpType.add
@@ -36,27 +35,20 @@ def tile_silknnue_b_kernel(tc, emb, w2, b2, w3, b3, w4, offs, out):
         w2_sb = held.tile([P, CB, H1], BF16, name="w2_sb")
         w3_sb = held.tile([P, 2 * MB, H2], BF16, name="w3_sb")
         w4_sb = held.tile([P, 2 * QB, M], BF16, name="w4_sb")
-        bias_rows = held.tile([P, P], F32, name="bias_rows")
-        nc.gpsimd.memset(bias_rows[:], 0.0)
+        bias = held.tile([P, MB + QB], F32, name="bias")
         for cb in range(CB):
             nc.sync.dma_start(tables[cb][:], emb[cb * P : (cb + 1) * P, :])
             if cb == LANES - 1:
                 nc.sync.dma_start(w2_sb[:], w2.rearrange("(cb p) m -> p cb m", p=P))
-                nc.sync.dma_start(bias_rows[0:MB, :], b2.rearrange("(mb p) o -> mb (p o)", p=P))
-                nc.sync.dma_start(bias_rows[MB : MB + QB, :], b3.rearrange("(qb p) o -> qb (p o)", p=P))
+                nc.sync.dma_start(bias[:, 0:MB], b2.rearrange("(mb p) o -> p (mb o)", p=P))
+                nc.sync.dma_start(bias[:, MB : MB + QB], b3.rearrange("(qb p) o -> p (qb o)", p=P))
         nc.sync.dma_start(w3_sb[:], w3.rearrange("(e p) q -> p e q", p=P))
         nc.sync.dma_start(w4_sb[:], w4.rearrange("(e p) o -> p e o", p=P))
 
         zeros = held.tile([P, WIDEST], F32, name="zeros")
         nc.gpsimd.memset(zeros[:], 0.0)
-        identity = held.tile([P, P], F32, name="identity")
-        make_identity(nc, identity[:])
-        flipped = psum.tile([P, BANK], F32, name="flipped", tag="bank")
-        nc.tensor.transpose(flipped[:, 0:P], bias_rows[:], identity[:])
-        bias = held.tile([P, MB + QB], F32, name="bias")
         neg_bias = held.tile([P, MB + QB], F32, name="neg_bias")
-        nc.scalar.copy(bias[:], flipped[:, 0 : MB + QB])
-        nc.scalar.mul(neg_bias[:], flipped[:, 0 : MB + QB], -1.0)
+        nc.scalar.mul(neg_bias[:], bias[:], -1.0)
 
         def layer1(h1, r, total, cb, c0, w):
             nc.scalar.activation(r[:, cb, :w], total[:, c0 : c0 + w], RELU)

@@ -45,7 +45,7 @@ def tile_silknnue_b_kernel(tc, emb, w2, b2, w3, b3, w4, offs, out):
         nc.sync.dma_start(w3_sb[:], w3.rearrange("(e p) q -> p e q", p=P))
         nc.sync.dma_start(w4_sb[:], w4.rearrange("(e p) o -> p e o", p=P))
 
-        zeros = held.tile([P, WIDEST], F32, name="zeros")
+        zeros = held.tile([P, B], F32, name="zeros")
         nc.gpsimd.memset(zeros[:], 0.0)
         neg_bias = held.tile([P, MB + QB], F32, name="neg_bias")
         nc.scalar.mul(neg_bias[:], bias[:], -1.0)
@@ -115,6 +115,9 @@ def tile_silknnue_b_kernel(tc, emb, w2, b2, w3, b3, w4, offs, out):
                     nc.scalar.copy(y_sb[:, :w], y[ob][:, :w])
                 nc.sync.dma_start(out[ob * P : (ob + 1) * P, p0 : p0 + w], y_sb[:, :w])
 
+        step0_of_block0 = held.tile([P, B], F32, name="step0_of_block0")
+        nc.vector.tensor_tensor(step0_of_block0[:], tables[0][:].indirect(offsets[:, 0 : B // 16]), zeros[:], ADD)
+
         p0 = 0
         for group in GROUPS:
             gw = sum(group)
@@ -124,17 +127,20 @@ def tile_silknnue_b_kernel(tc, emb, w2, b2, w3, b3, w4, offs, out):
             totals = {}
             for cb0 in range(0, CB, LANES):
                 lanes = range(cb0, cb0 + LANES)
-                acc = {cb: zeros for cb in lanes}
+                acc = {cb: zeros[:, :gw] for cb in lanes}
                 for k in range(K):
                     first = (k * B + p0) // 16
                     for cb in lanes:
+                        if k == 0 and cb == 0:
+                            acc[cb] = step0_of_block0[:, p0 : p0 + gw]
+                            continue
                         picked = tables[cb][:].indirect(offsets[:, first : first + gw // 16])
                         if k < K - 1:
                             longer = steps.tile([P, WIDEST], F32, name="partial")
                         else:
                             longer = sums.tile([P, WIDEST], F32, name="total")
-                        nc.vector.tensor_tensor(longer[:, :gw], picked, acc[cb][:, :gw], ADD)
-                        acc[cb] = longer
+                        nc.vector.tensor_tensor(longer[:, :gw], picked, acc[cb], ADD)
+                        acc[cb] = longer[:, :gw]
                 for cb in lanes:
                     totals[cb] = acc[cb]
                     layer1(h1, r, totals[cb], cb, 0, group[0])

@@ -50,16 +50,14 @@ def tile_silknnue_b_kernel(tc, emb, w2, b2, w3, b3, w4, offs, out):
         neg_bias = held.tile([P, MB + QB], F32, name="neg_bias")
         nc.scalar.mul(neg_bias[:], bias[:], -1.0)
 
-        def layer1(h1, r, total, cb, c0, w):
-            nc.scalar.activation(r[:, cb, :w], total[:, c0 : c0 + w], RELU)
-            for mb in range(MB):
-                nc.tensor.matmul(
-                    h1[mb][:, :w],
-                    w2_sb[:, cb, mb * P : (mb + 1) * P],
-                    r[:, cb, :w],
-                    start=(cb == 0),
-                    stop=(cb == CB - 1),
-                )
+        def layer1(h1, r, cb, mb, w):
+            nc.tensor.matmul(
+                h1[mb][:, :w],
+                w2_sb[:, cb, mb * P : (mb + 1) * P],
+                r[:, cb, :w],
+                start=(cb == 0),
+                stop=(cb == CB - 1),
+            )
 
         def paired_relu(pos, neg, bank, j, w):
             nc.scalar.activation(pos[:, :w], bank[:, :w], RELU, bias=bias[:, j : j + 1], scale=1.0)
@@ -143,7 +141,9 @@ def tile_silknnue_b_kernel(tc, emb, w2, b2, w3, b3, w4, offs, out):
                         acc[cb] = longer[:, :gw]
                 for cb in lanes:
                     totals[cb] = acc[cb]
-                    layer1(h1, r, totals[cb], cb, 0, group[0])
+                    nc.scalar.activation(r[:, cb, : group[0]], totals[cb][:, : group[0]], RELU)
+                    for mb in range(MB):
+                        layer1(h1, r, cb, mb, group[0])
             after_layer1(h1, p0, group[0])
 
             c0 = group[0]
@@ -151,7 +151,10 @@ def tile_silknnue_b_kernel(tc, emb, w2, b2, w3, b3, w4, offs, out):
                 h1 = [psum.tile([P, BANK], F32, name=f"h1_{mb}", tag="bank") for mb in range(MB)]
                 r = turns.tile([P, CB, BANK], BF16, name="r", tag="turn")
                 for cb in range(CB):
-                    layer1(h1, r, totals[cb], cb, c0, w)
+                    nc.scalar.activation(r[:, cb, :w], totals[cb][:, c0 : c0 + w], RELU)
+                for mb in range(MB):
+                    for cb in range(CB):
+                        layer1(h1, r, cb, mb, w)
                 after_layer1(h1, p0 + c0, w)
                 c0 += w
             p0 += gw

@@ -15,6 +15,7 @@ GROUPS = ((512, 96), (288,), (128,))
 WIDEST = max(sum(group) for group in GROUPS)
 assert sum(sum(group) for group in GROUPS) == B and max(max(group) for group in GROUPS) <= BANK
 LANES = 2
+IN_A_BANK = 4
 
 FLOPS = 2 * B * (C * H1 + 2 * H1 * H2 + 2 * H2 * M)
 
@@ -111,7 +112,8 @@ def tile_silknnue_b_kernel(tc, emb, w2, b2, w3, b3, w4, offs, out):
                     nc.vector.tensor_copy(y_sb[:, :w], y[ob][:, :w])
                 else:
                     nc.scalar.copy(y_sb[:, :w], y[ob][:, :w])
-                nc.sync.dma_start(out[ob * P : (ob + 1) * P, p0 : p0 + w], y_sb[:, :w])
+                store_queue = nc.sync if ob == 0 else nc.scalar
+                store_queue.dma_start(out[ob * P : (ob + 1) * P, p0 : p0 + w], y_sb[:, :w])
 
         step0_of_block0 = held.tile([P, B], F32, name="step0_of_block0")
         nc.vector.tensor_tensor(step0_of_block0[:], tables[0][:].indirect(offsets[:, 0 : B // 16]), zeros[:], ADD)
@@ -148,13 +150,24 @@ def tile_silknnue_b_kernel(tc, emb, w2, b2, w3, b3, w4, offs, out):
 
             c0 = group[0]
             for w in group[1:]:
-                h1 = [psum.tile([P, BANK], F32, name=f"h1_{mb}", tag="bank") for mb in range(MB)]
-                r = turns.tile([P, CB, BANK], BF16, name="r", tag="turn")
+                assert w * IN_A_BANK <= BANK
+                h1 = []
+                r = held.tile([P, CB, w], BF16, name="r_further")
                 for cb in range(CB):
-                    nc.scalar.activation(r[:, cb, :w], totals[cb][:, c0 : c0 + w], RELU)
-                for mb in range(MB):
-                    for cb in range(CB):
-                        layer1(h1, r, cb, mb, w)
+                    nc.scalar.activation(r[:, cb, :], totals[cb][:, c0 : c0 + w], RELU)
+                for mb0 in range(0, MB, IN_A_BANK):
+                    bank = psum.tile([P, BANK], F32, name="h1_side_by_side", tag="bank")
+                    for mb in range(mb0, mb0 + IN_A_BANK):
+                        column = (mb - mb0) * w
+                        h1.append(bank[:, column : column + w])
+                        for cb in range(CB):
+                            nc.tensor.matmul(
+                                h1[mb],
+                                w2_sb[:, cb, mb * P : (mb + 1) * P],
+                                r[:, cb, :],
+                                start=(mb == mb0 and cb == 0),
+                                stop=(mb == mb0 + IN_A_BANK - 1 and cb == CB - 1),
+                            )
                 after_layer1(h1, p0 + c0, w)
                 c0 += w
             p0 += gw

@@ -11,11 +11,12 @@ N = K * B
 BANK = 512
 CB, MB, QB, OB = C // P, H1 // P, H2 // P, M // P
 
-GROUPS = ((512, 96), (288,), (128,))
+GROUPS = ((512, 128), (288,), (96,))
 WIDEST = max(sum(group) for group in GROUPS)
 assert sum(sum(group) for group in GROUPS) == B and max(max(group) for group in GROUPS) <= BANK
-LANES = 2
+LANES = (2, 2, 3)
 IN_A_BANK = 4
+EARLY = 3
 
 FLOPS = 2 * B * (C * H1 + 2 * H1 * H2 + 2 * H2 * M)
 
@@ -24,10 +25,11 @@ def tile_silknnue_b_kernel(tc, emb, w2, b2, w3, b3, w4, offs, out):
     nc = tc.nc
     with (
         tc.tile_pool(name="held", bufs=1) as held,
-        tc.tile_pool(name="steps", bufs=3 * LANES) as steps,
+        tc.tile_pool(name="steps", bufs=3 * max(LANES)) as steps,
         tc.tile_pool(name="sums", bufs=2 * CB) as sums,
         tc.tile_pool(name="acts", bufs=2) as acts,
         tc.tile_pool(name="turns", bufs=1) as turns,
+        tc.tile_pool(name="ties", bufs=1) as ties,
         tc.psum_pool(name="psum", bufs=8) as psum,
     ):
         offsets = held.tile([P, N // 16], U16, name="offsets")
@@ -39,7 +41,7 @@ def tile_silknnue_b_kernel(tc, emb, w2, b2, w3, b3, w4, offs, out):
         bias = held.tile([P, MB + QB], F32, name="bias")
         for cb in range(CB):
             nc.sync.dma_start(tables[cb][:], emb[cb * P : (cb + 1) * P, :])
-            if cb == LANES - 1:
+            if cb == LANES[0] - 1:
                 nc.sync.dma_start(w2_sb[:], w2.rearrange("(cb p) m -> p cb m", p=P))
                 nc.sync.dma_start(bias[:, 0:MB], b2.rearrange("(mb p) o -> p (mb o)", p=P))
                 nc.sync.dma_start(bias[:, MB : MB + QB], b3.rearrange("(qb p) o -> p (qb o)", p=P))
@@ -51,21 +53,13 @@ def tile_silknnue_b_kernel(tc, emb, w2, b2, w3, b3, w4, offs, out):
         neg_bias = held.tile([P, MB + QB], F32, name="neg_bias")
         nc.scalar.mul(neg_bias[:], bias[:], -1.0)
 
-        def layer1(h1, r, cb, mb, w):
-            nc.tensor.matmul(
-                h1[mb][:, :w],
-                w2_sb[:, cb, mb * P : (mb + 1) * P],
-                r[:, cb, :w],
-                start=(cb == 0),
-                stop=(cb == CB - 1),
-            )
-
         def paired_relu(pos, neg, bank, j, w):
             nc.scalar.activation(pos[:, :w], bank[:, :w], RELU, bias=bias[:, j : j + 1], scale=1.0)
             nc.scalar.activation(neg[:, :w], bank[:, :w], RELU, bias=neg_bias[:, j : j + 1], scale=-1.0)
 
         def after_layer1(h1, p0, w):
-            u1 = [acts.tile([P, BANK], BF16, name=f"u1_{e}") for e in range(2 * MB)]
+            u1 = [acts.tile([P, BANK], BF16, name=f"u1_{e}") for e in range(2 * MB - 1)]
+            u1.append(ties.tile([P, EARLY, BANK], BF16, name="u1_last", tag="early")[:, 0, :])
             for mb in range(MB):
                 paired_relu(u1[mb], u1[MB + mb], h1[mb], mb, w)
 
@@ -112,21 +106,26 @@ def tile_silknnue_b_kernel(tc, emb, w2, b2, w3, b3, w4, offs, out):
                     nc.vector.tensor_copy(y_sb[:, :w], y[ob][:, :w])
                 else:
                     nc.scalar.copy(y_sb[:, :w], y[ob][:, :w])
-                store_queue = nc.sync if ob == 0 else nc.scalar
+                store_queue = nc.scalar if p0 + w == B and ob == 1 else nc.sync
                 store_queue.dma_start(out[ob * P : (ob + 1) * P, p0 : p0 + w], y_sb[:, :w])
 
         step0_of_block0 = held.tile([P, B], F32, name="step0_of_block0")
         nc.vector.tensor_tensor(step0_of_block0[:], tables[0][:].indirect(offsets[:, 0 : B // 16]), zeros[:], ADD)
 
         p0 = 0
-        for group in GROUPS:
+        for group, lane_count in zip(GROUPS, LANES):
             gw = sum(group)
 
-            h1 = [psum.tile([P, BANK], F32, name=f"h1_{mb}", tag="bank") for mb in range(MB)]
+            in_a_bank = BANK // group[0]
+            banks = [psum.tile([P, BANK], F32, name=f"h1_bank{b}", tag="bank") for b in range(MB // min(in_a_bank, 4))]
+            in_a_bank = MB // len(banks)
+            h1 = [banks[mb // in_a_bank][:, (mb % in_a_bank) * group[0] :] for mb in range(MB)]
             r = turns.tile([P, CB, BANK], BF16, name="r", tag="turn")
+            if p0 > 0:
+                r_early = ties.tile([P, EARLY, BANK], BF16, name="r_early", tag="early")
             totals = {}
-            for cb0 in range(0, CB, LANES):
-                lanes = range(cb0, cb0 + LANES)
+            for cb0 in range(0, CB, lane_count):
+                lanes = range(cb0, min(cb0 + lane_count, CB))
                 acc = {cb: zeros[:, :gw] for cb in lanes}
                 for k in range(K):
                     first = (k * B + p0) // 16
@@ -143,9 +142,16 @@ def tile_silknnue_b_kernel(tc, emb, w2, b2, w3, b3, w4, offs, out):
                         acc[cb] = longer[:, :gw]
                 for cb in lanes:
                     totals[cb] = acc[cb]
-                    nc.scalar.activation(r[:, cb, : group[0]], totals[cb][:, : group[0]], RELU)
+                    r_cb = r_early if p0 > 0 and cb < EARLY else r
+                    nc.scalar.activation(r_cb[:, cb, : group[0]], totals[cb][:, : group[0]], RELU)
                     for mb in range(MB):
-                        layer1(h1, r, cb, mb, group[0])
+                        nc.tensor.matmul(
+                            h1[mb][:, : group[0]],
+                            w2_sb[:, cb, mb * P : (mb + 1) * P],
+                            r_cb[:, cb, : group[0]],
+                            start=(cb == 0 and mb % in_a_bank == 0),
+                            stop=(cb == CB - 1 and mb % in_a_bank == in_a_bank - 1),
+                        )
             after_layer1(h1, p0, group[0])
 
             c0 = group[0]

@@ -17,6 +17,8 @@ assert sum(sum(group) for group in GROUPS) == B and max(max(group) for group in 
 LANES = (2, 2, 3)
 IN_A_BANK = 4
 EARLY = 3
+LATE_STEP = (3, None, None)
+TOGETHER = 5
 
 FLOPS = 2 * B * (C * H1 + 2 * H1 * H2 + 2 * H2 * M)
 
@@ -113,8 +115,9 @@ def tile_silknnue_b_kernel(tc, emb, w2, b2, w3, b3, w4, offs, out):
         nc.vector.tensor_tensor(step0_of_block0[:], tables[0][:].indirect(offsets[:, 0 : B // 16]), zeros[:], ADD)
 
         p0 = 0
-        for group, lane_count in zip(GROUPS, LANES):
+        for group, lane_count, late_step in zip(GROUPS, LANES, LATE_STEP):
             gw = sum(group)
+            chunks = [(sum(group[:i]), w) for i, w in enumerate(group)]
 
             in_a_bank = BANK // group[0]
             banks = [psum.tile([P, BANK], F32, name=f"h1_bank{b}", tag="bank") for b in range(MB // min(in_a_bank, 4))]
@@ -124,34 +127,63 @@ def tile_silknnue_b_kernel(tc, emb, w2, b2, w3, b3, w4, offs, out):
             if p0 > 0:
                 r_early = ties.tile([P, EARLY, BANK], BF16, name="r_early", tag="early")
             totals = {}
-            for cb0 in range(0, CB, lane_count):
-                lanes = range(cb0, min(cb0 + lane_count, CB))
-                acc = {cb: zeros[:, :gw] for cb in lanes}
-                for k in range(K):
-                    first = (k * B + p0) // 16
+            lane_sets = [range(cb0, min(cb0 + lane_count, CB)) for cb0 in range(0, CB, lane_count)]
+            r_of = {cb: r_early[:, cb, :] if p0 > 0 and cb < EARLY else r[:, cb, :] for cb in range(CB)}
+
+            def add_steps(acc, lanes, k0, k1, lo, hi):
+                for k in range(k0, k1):
+                    first = (k * B + p0 + lo) // 16
                     for cb in lanes:
                         if k == 0 and cb == 0:
-                            acc[cb] = step0_of_block0[:, p0 : p0 + gw]
+                            acc[cb] = step0_of_block0[:, p0 + lo : p0 + hi]
                             continue
-                        picked = tables[cb][:].indirect(offsets[:, first : first + gw // 16])
-                        if k < K - 1:
-                            longer = steps.tile([P, WIDEST], F32, name="partial")
-                        else:
+                        picked = tables[cb][:].indirect(offsets[:, first : first + (hi - lo) // 16])
+                        if k == K - 1:
                             longer = sums.tile([P, WIDEST], F32, name="total")
-                        nc.vector.tensor_tensor(longer[:, :gw], picked, acc[cb], ADD)
-                        acc[cb] = longer[:, :gw]
+                        elif k == late_step and cb == CB - 1:
+                            longer = ties.tile([P, WIDEST], F32, name="late_partial", tag="late")
+                        else:
+                            longer = steps.tile([P, WIDEST], F32, name="partial")
+                        nc.vector.tensor_tensor(longer[:, : hi - lo], picked, acc[cb], ADD)
+                        acc[cb] = longer[:, : hi - lo]
+
+            def sum_up(lanes, together=K):
+                acc = {cb: zeros[:, :gw] for cb in lanes}
+                add_steps(acc, lanes, 0, together, 0, gw)
+                cuts = [0, gw] if together == K else [0, group[0], gw]
+                for lo, hi in zip(cuts[:-1], cuts[1:]):
+                    part = {cb: acc[cb][:, lo:hi] for cb in lanes}
+                    add_steps(part, lanes, together, K, lo, hi)
+                    for cb in lanes:
+                        for c, w in chunks:
+                            if lo <= c < hi:
+                                totals[cb, c] = part[cb][:, c - lo : c - lo + w]
+
+            def feed_layer1(lanes):
                 for cb in lanes:
-                    totals[cb] = acc[cb]
-                    r_cb = r_early if p0 > 0 and cb < EARLY else r
-                    nc.scalar.activation(r_cb[:, cb, : group[0]], totals[cb][:, : group[0]], RELU)
+                    nc.scalar.activation(r_of[cb][:, : group[0]], totals[cb, 0], RELU)
                     for mb in range(MB):
                         nc.tensor.matmul(
                             h1[mb][:, : group[0]],
                             w2_sb[:, cb, mb * P : (mb + 1) * P],
-                            r_cb[:, cb, : group[0]],
+                            r_of[cb][:, : group[0]],
                             start=(cb == 0 and mb % in_a_bank == 0),
                             stop=(cb == CB - 1 and mb % in_a_bank == in_a_bank - 1),
                         )
+
+            for lanes in lane_sets[:-2]:
+                sum_up(lanes)
+                feed_layer1(lanes)
+            sum_up(lane_sets[-2])
+            if late_step is None:
+                feed_layer1(lane_sets[-2])
+            sum_up(lane_sets[-1], K if len(group) == 1 else TOGETHER)
+            if late_step is not None:
+                r_late = ties.tile([P, WIDEST // BANK + 1, BANK], BF16, name="r_late", tag="late")
+                for i, cb in enumerate(lane_sets[-2]):
+                    r_of[cb] = r_late[:, i, :]
+                feed_layer1(lane_sets[-2])
+            feed_layer1(lane_sets[-1])
             after_layer1(h1, p0, group[0])
 
             c0 = group[0]
@@ -160,7 +192,7 @@ def tile_silknnue_b_kernel(tc, emb, w2, b2, w3, b3, w4, offs, out):
                 h1 = []
                 r = held.tile([P, CB, w], BF16, name="r_further")
                 for cb in range(CB):
-                    nc.scalar.activation(r[:, cb, :], totals[cb][:, c0 : c0 + w], RELU)
+                    nc.scalar.activation(r[:, cb, :], totals[cb, c0], RELU)
                 for mb0 in range(0, MB, IN_A_BANK):
                     bank = psum.tile([P, BANK], F32, name="h1_side_by_side", tag="bank")
                     for mb in range(mb0, mb0 + IN_A_BANK):

@@ -108,8 +108,7 @@ def tile_silknnue_b_kernel(tc, emb, w2, b2, w3, b3, w4, offs, out):
                     nc.vector.tensor_copy(y_sb[:, :w], y[ob][:, :w])
                 else:
                     nc.scalar.copy(y_sb[:, :w], y[ob][:, :w])
-                store_queue = nc.scalar if p0 + w == B and ob == 1 else nc.sync
-                store_queue.dma_start(out[ob * P : (ob + 1) * P, p0 : p0 + w], y_sb[:, :w])
+                nc.sync.dma_start(out[ob * P : (ob + 1) * P, p0 : p0 + w], y_sb[:, :w])
 
         step0_of_block0 = held.tile([P, B], F32, name="step0_of_block0")
         nc.vector.tensor_tensor(step0_of_block0[:], tables[0][:].indirect(offsets[:, 0 : B // 16]), zeros[:], ADD)

@@ -18,7 +18,7 @@ LANES = (2, 2, 3)
 IN_A_BANK = 4
 EARLY = 3
 LATE_STEP = (3, None, None)
-TOGETHER = 5
+TOGETHER = 7
 
 FLOPS = 2 * B * (C * H1 + 2 * H1 * H2 + 2 * H2 * M)
 
@@ -119,7 +119,7 @@ def tile_silknnue_b_kernel(tc, emb, w2, b2, w3, b3, w4, offs, out):
             chunks = [(sum(group[:i]), w) for i, w in enumerate(group)]
 
             in_a_bank = BANK // group[0]
-            banks = [psum.tile([P, BANK], F32, name=f"h1_bank{b}", tag="bank") for b in range(MB // min(in_a_bank, 4))]
+            banks = [psum.tile([P, BANK], F32, name=f"h1_bank{b}", tag="bank") for b in range(MB // min(in_a_bank, 2))]
             in_a_bank = MB // len(banks)
             h1 = [banks[mb // in_a_bank][:, (mb % in_a_bank) * group[0] :] for mb in range(MB)]
             r = turns.tile([P, CB, BANK], BF16, name="r", tag="turn")

@@ -16,7 +16,7 @@ WIDEST = max(sum(group) for group in GROUPS)
 assert sum(sum(group) for group in GROUPS) == B and max(max(group) for group in GROUPS) <= BANK
 LANES = (2, 2, 3)
 IN_A_BANK = 4
-EARLY = 3
+EARLY = 6
 LATE_STEP = (3, None, None)
 TOGETHER = 7
 

@@ -17,8 +17,7 @@ assert sum(sum(group) for group in GROUPS) == B and max(max(group) for group in 
 LANES = (2, 2, 3)
 IN_A_BANK = 4
 EARLY = 6
-LATE_STEP = (3, None, None)
-TOGETHER = 7
+LATE_STEP = (4, None, None)
 
 FLOPS = 2 * B * (C * H1 + 2 * H1 * H2 + 2 * H2 * M)
 
@@ -139,24 +138,19 @@ def tile_silknnue_b_kernel(tc, emb, w2, b2, w3, b3, w4, offs, out):
                         picked = tables[cb][:].indirect(offsets[:, first : first + (hi - lo) // 16])
                         if k == K - 1:
                             longer = sums.tile([P, WIDEST], F32, name="total")
-                        elif k == late_step and cb == CB - 1:
+                        elif k == late_step and cb == CB - 2:
                             longer = ties.tile([P, WIDEST], F32, name="late_partial", tag="late")
                         else:
                             longer = steps.tile([P, WIDEST], F32, name="partial")
                         nc.vector.tensor_tensor(longer[:, : hi - lo], picked, acc[cb], ADD)
                         acc[cb] = longer[:, : hi - lo]
 
-            def sum_up(lanes, together=K):
+            def sum_up(lanes):
                 acc = {cb: zeros[:, :gw] for cb in lanes}
-                add_steps(acc, lanes, 0, together, 0, gw)
-                cuts = [0, gw] if together == K else [0, group[0], gw]
-                for lo, hi in zip(cuts[:-1], cuts[1:]):
-                    part = {cb: acc[cb][:, lo:hi] for cb in lanes}
-                    add_steps(part, lanes, together, K, lo, hi)
-                    for cb in lanes:
-                        for c, w in chunks:
-                            if lo <= c < hi:
-                                totals[cb, c] = part[cb][:, c - lo : c - lo + w]
+                add_steps(acc, lanes, 0, K, 0, gw)
+                for cb in lanes:
+                    for c, w in chunks:
+                        totals[cb, c] = acc[cb][:, c : c + w]
 
             def feed_layer1(lanes):
                 for cb in lanes:
@@ -176,7 +170,7 @@ def tile_silknnue_b_kernel(tc, emb, w2, b2, w3, b3, w4, offs, out):
             sum_up(lane_sets[-2])
             if late_step is None:
                 feed_layer1(lane_sets[-2])
-            sum_up(lane_sets[-1], K if len(group) == 1 else TOGETHER)
+            sum_up(lane_sets[-1])
             if late_step is not None:
                 r_late = ties.tile([P, WIDEST // BANK + 1, BANK], BF16, name="r_late", tag="late")
                 for i, cb in enumerate(lane_sets[-2]):

import concourse.mybir as mybir

F32, BF16, U16 = mybir.dt.float32, mybir.dt.bfloat16, mybir.dt.uint16
ADD = mybir.AluOpType.add
RELU = mybir.ActivationFunctionType.Relu

P = 128
C, S, K, B = 1024, 2048, 8, 1024
H1, H2, M = 1024, 512, 256
N = K * B
BANK = 512
CB, MB, QB, OB = C // P, H1 // P, H2 // P, M // P

GROUPS = ((512, 128), (288,), (96,))
WIDEST = max(sum(group) for group in GROUPS)
assert sum(sum(group) for group in GROUPS) == B and max(max(group) for group in GROUPS) <= BANK
LANES = (2, 2, 3)
IN_A_BANK = 4
EARLY = 6
LATE_STEP = (4, None, None)

FLOPS = 2 * B * (C * H1 + 2 * H1 * H2 + 2 * H2 * M)


def tile_silknnue_b_kernel(tc, emb, w2, b2, w3, b3, w4, offs, out):
    nc = tc.nc
    with (
        tc.tile_pool(name="held", bufs=1) as held,
        tc.tile_pool(name="steps", bufs=3 * max(LANES)) as steps,
        tc.tile_pool(name="sums", bufs=2 * CB) as sums,
        tc.tile_pool(name="acts", bufs=2) as acts,
        tc.tile_pool(name="turns", bufs=1) as turns,
        tc.tile_pool(name="ties", bufs=1) as ties,
        tc.psum_pool(name="psum", bufs=8) as psum,
    ):
        offsets = held.tile([P, N // 16], U16, name="offsets")
        nc.sync.dma_start(offsets[:], offs)
        tables = [held.tile([P, S], F32, name=f"table{cb}") for cb in range(CB)]
        w2_sb = held.tile([P, CB, H1], BF16, name="w2_sb")
        w3_sb = held.tile([P, 2 * MB, H2], BF16, name="w3_sb")
        w4_sb = held.tile([P, 2 * QB, M], BF16, name="w4_sb")
        bias = held.tile([P, MB + QB], F32, name="bias")
        for cb in range(CB):
            nc.sync.dma_start(tables[cb][:], emb[cb * P : (cb + 1) * P, :])
            if cb == LANES[0] - 1:
                nc.sync.dma_start(w2_sb[:], w2.rearrange("(cb p) m -> p cb m", p=P))
                nc.sync.dma_start(bias[:, 0:MB], b2.rearrange("(mb p) o -> p (mb o)", p=P))
                nc.sync.dma_start(bias[:, MB : MB + QB], b3.rearrange("(qb p) o -> p (qb o)", p=P))
        nc.sync.dma_start(w3_sb[:], w3.rearrange("(e p) q -> p e q", p=P))
        nc.sync.dma_start(w4_sb[:], w4.rearrange("(e p) o -> p e o", p=P))

        zeros = held.tile([P, B], F32, name="zeros")
        nc.gpsimd.memset(zeros[:], 0.0)
        neg_bias = held.tile([P, MB + QB], F32, name="neg_bias")
        nc.scalar.mul(neg_bias[:], bias[:], -1.0)

        def paired_relu(pos, neg, bank, j, w):
            nc.scalar.activation(pos[:, :w], bank[:, :w], RELU, bias=bias[:, j : j + 1], scale=1.0)
            nc.scalar.activation(neg[:, :w], bank[:, :w], RELU, bias=neg_bias[:, j : j + 1], scale=-1.0)

        def after_layer1(h1, p0, w):
            u1 = [acts.tile([P, BANK], BF16, name=f"u1_{e}") for e in range(2 * MB - 1)]
            u1.append(ties.tile([P, EARLY, BANK], BF16, name="u1_last", tag="early")[:, 0, :])
            for mb in range(MB):
                paired_relu(u1[mb], u1[MB + mb], h1[mb], mb, w)

            u2 = turns.tile([P, 2 * QB, BANK], BF16, name="u2", tag="turn")
            ready_order = [e for mb in range(MB) for e in (mb, MB + mb)]
            h2 = {}

            def layer2(e, qb):
                nc.tensor.matmul(
                    h2[qb][:, :w],
                    w3_sb[:, e, qb * P : (qb + 1) * P],
                    u1[e][:, :w],
                    start=(e == ready_order[0]),
                    stop=(e == ready_order[-1]),
                )

            for qb in range(0, QB // 2):
                h2[qb] = psum.tile([P, BANK], F32, name=f"h2_{qb}", tag="bank")
            for e in ready_order:
                for qb in range(0, QB // 2):
                    layer2(e, qb)
            for qb in range(0, QB // 2):
                paired_relu(u2[:, qb, :], u2[:, QB + qb, :], h2[qb], MB + qb, w)
            for qb in range(QB // 2, QB):
                h2[qb] = psum.tile([P, BANK], F32, name=f"h2_{qb}", tag="bank")
                for e in ready_order:
                    layer2(e, qb)
                paired_relu(u2[:, qb, :], u2[:, QB + qb, :], h2[qb], MB + qb, w)

            y = [psum.tile([P, BANK], F32, name=f"y{ob}", tag="bank") for ob in range(OB)]
            for qb in range(QB):
                for e in (qb, QB + qb):
                    for ob in range(OB):
                        nc.tensor.matmul(
                            y[ob][:, :w],
                            w4_sb[:, e, ob * P : (ob + 1) * P],
                            u2[:, e, :w],
                            start=(e == 0),
                            stop=(e == 2 * QB - 1),
                        )
            for ob in range(OB):
                y_sb = acts.tile([P, BANK], F32, name=f"y_sb{ob}")
                if p0 + w == B and ob == 0:
                    nc.vector.tensor_copy(y_sb[:, :w], y[ob][:, :w])
                else:
                    nc.scalar.copy(y_sb[:, :w], y[ob][:, :w])
                nc.sync.dma_start(out[ob * P : (ob + 1) * P, p0 : p0 + w], y_sb[:, :w])

        step0_of_block0 = held.tile([P, B], F32, name="step0_of_block0")
        nc.vector.tensor_tensor(step0_of_block0[:], tables[0][:].indirect(offsets[:, 0 : B // 16]), zeros[:], ADD)

        p0 = 0
        for group, lane_count, late_step in zip(GROUPS, LANES, LATE_STEP):
            gw = sum(group)
            chunks = [(sum(group[:i]), w) for i, w in enumerate(group)]

            in_a_bank = BANK // group[0]
            banks = [psum.tile([P, BANK], F32, name=f"h1_bank{b}", tag="bank") for b in range(MB // min(in_a_bank, 2))]
            in_a_bank = MB // len(banks)
            h1 = [banks[mb // in_a_bank][:, (mb % in_a_bank) * group[0] :] for mb in range(MB)]
            r = turns.tile([P, CB, BANK], BF16, name="r", tag="turn")
            if p0 > 0:
                r_early = ties.tile([P, EARLY, BANK], BF16, name="r_early", tag="early")
            totals = {}
            lane_sets = [range(cb0, min(cb0 + lane_count, CB)) for cb0 in range(0, CB, lane_count)]
            r_of = {cb: r_early[:, cb, :] if p0 > 0 and cb < EARLY else r[:, cb, :] for cb in range(CB)}

            def add_steps(acc, lanes, k0, k1, lo, hi):
                for k in range(k0, k1):
                    first = (k * B + p0 + lo) // 16
                    for cb in lanes:
                        if k == 0 and cb == 0:
                            acc[cb] = step0_of_block0[:, p0 + lo : p0 + hi]
                            continue
                        picked = tables[cb][:].indirect(offsets[:, first : first + (hi - lo) // 16])
                        if k == K - 1:
                            longer = sums.tile([P, WIDEST], F32, name="total")
                        elif k == late_step and cb == CB - 2:
                            longer = ties.tile([P, WIDEST], F32, name="late_partial", tag="late")
                        else:
                            longer = steps.tile([P, WIDEST], F32, name="partial")
                        nc.vector.tensor_tensor(longer[:, : hi - lo], picked, acc[cb], ADD)
                        acc[cb] = longer[:, : hi - lo]

            def sum_up(lanes):
                acc = {cb: zeros[:, :gw] for cb in lanes}
                add_steps(acc, lanes, 0, K, 0, gw)
                for cb in lanes:
                    for c, w in chunks:
                        totals[cb, c] = acc[cb][:, c : c + w]

            def feed_layer1(lanes):
                for cb in lanes:
                    nc.scalar.activation(r_of[cb][:, : group[0]], totals[cb, 0], RELU)
                    for mb in range(MB):
                        nc.tensor.matmul(
                            h1[mb][:, : group[0]],
                            w2_sb[:, cb, mb * P : (mb + 1) * P],
                            r_of[cb][:, : group[0]],
                            start=(cb == 0 and mb % in_a_bank == 0),
                            stop=(cb == CB - 1 and mb % in_a_bank == in_a_bank - 1),
                        )

            for lanes in lane_sets[:-2]:
                sum_up(lanes)
                feed_layer1(lanes)
            sum_up(lane_sets[-2])
            if late_step is None:
                feed_layer1(lane_sets[-2])
            sum_up(lane_sets[-1])
            if late_step is not None:
                r_late = ties.tile([P, WIDEST // BANK + 1, BANK], BF16, name="r_late", tag="late")
                for i, cb in enumerate(lane_sets[-2]):
                    r_of[cb] = r_late[:, i, :]
                feed_layer1(lane_sets[-2])
            feed_layer1(lane_sets[-1])
            after_layer1(h1, p0, group[0])

            c0 = group[0]
            for w in group[1:]:
                assert w * IN_A_BANK <= BANK
                h1 = []
                r = held.tile([P, CB, w], BF16, name="r_further")
                for cb in range(CB):
                    nc.scalar.activation(r[:, cb, :], totals[cb, c0], RELU)
                for mb0 in range(0, MB, IN_A_BANK):
                    bank = psum.tile([P, BANK], F32, name="h1_side_by_side", tag="bank")
                    for mb in range(mb0, mb0 + IN_A_BANK):
                        column = (mb - mb0) * w
                        h1.append(bank[:, column : column + w])
                        for cb in range(CB):
                            nc.tensor.matmul(
                                h1[mb],
                                w2_sb[:, cb, mb * P : (mb + 1) * P],
                                r[:, cb, :],
                                start=(mb == mb0 and cb == 0),
                                stop=(mb == mb0 + IN_A_BANK - 1 and cb == CB - 1),
                            )
                after_layer1(h1, p0 + c0, w)
                c0 += w
            p0 += gw
